import numpy as np
import ml_dtypes


def mxq(x, axis, fmt="e4m3"):
    dtype, down = {"e4m3": (ml_dtypes.float8_e4m3fn, 7), "e5m2": (ml_dtypes.float8_e5m2, 14)}[fmt]
    v = np.moveaxis(np.asarray(x, np.float32).astype(ml_dtypes.bfloat16).astype(np.float64), axis, -1)
    blocks = v.reshape(v.shape[:-1] + (-1, 32))
    amax = np.abs(blocks).max(-1, keepdims=True)
    byte = np.maximum(np.where(amax > 0, np.frexp(amax)[1] - 1 + 127, 0) - down, 1)
    scale = np.exp2(byte - 127.0)
    codes = (blocks / scale).astype(np.float32).astype(dtype).astype(np.float64)
    return np.moveaxis((codes * scale).reshape(v.shape), -1, axis)


WIDE = False


def mx_kscale(k):
    if not WIDE:
        return np.ones(k)
    levels = np.array([10, -10, 5, -5, 0])
    a = np.random.permutation(np.resize(levels, k // 512 * 4)).reshape(k // 512, 4)
    idx = np.arange(k)
    return np.exp2(a[idx // 512, idx % 128 // 32])


BF16 = ml_dtypes.bfloat16


def bf(x):
    return np.asarray(x, np.float32).astype(BF16)


def f64(x):
    return np.asarray(x).astype(np.float64)


B, H, L, D, C = 8, 4, 512, 128, 512


def decay_block(i0, n):
    head_idx = np.arange(H, dtype=np.float64)
    gamma = 1.0 - np.exp2(-5.0 - head_idx)
    log2_gamma = np.log2(gamma)
    pos_diff = np.arange(i0, i0 + C, dtype=np.float64)[:, None] - np.arange(n, dtype=np.float64)[None, :]
    causal = np.where(pos_diff >= 0, 1.0, 0.0)
    return np.exp2(pos_diff[None] * log2_gamma[:, None, None]) * causal[None]


def setup_inputs():
    s = mx_kscale(L)
    return {"q_scaled": bf(np.random.standard_normal((B, H, L, D)) / np.sqrt(D)),
            "k": bf(np.random.standard_normal((B, H, L, D)) * s[:, None]),
            "v": bf(np.random.standard_normal((B, H, L, D)) * 0.25 / s[:, None])}


def reference(q_scaled, k, v):
    vq = mxq(f64(v), 2, "e4m3")
    out = np.zeros((B, H, L, D))
    for i0 in range(0, L, C):
        n = i0 + C
        scores = f64(q_scaled)[:, :, i0:n] @ f64(k)[:, :, :n].transpose(0, 1, 3, 2)
        p = scores * decay_block(i0, n)[None]
        out[:, :, i0:n] = mxq(p, 3, "e4m3") @ vq[:, :, :n]
    return out

@@ -1,0 +1,192 @@
+import math
+from contextlib import ExitStack
+
+import concourse.mybir as mybir
+from concourse.masks import make_identity
+
+B, H, L, D = 8, 4, 512, 128
+P = 128
+NH = B * H
+FLOPS = 4 * B * H * L * L * D
+
+BF16 = mybir.dt.bfloat16
+F32 = mybir.dt.float32
+I32 = mybir.dt.int32
+U32 = mybir.dt.uint32
+U8 = mybir.dt.uint8
+FP8X4 = mybir.dt.float8_e4m3fn_x4
+ALU = mybir.AluOpType
+ACT = mybir.ActivationFunctionType
+
+S_PLACE = {3: (0, 0), 2: (1, 0), 0: (1, 3), 1: (2, 0)}
+NG = 3
+AHEAD = 3
+
+
+def tile_model_pa_t_kernel(tc, q_scaled, k, v, out):
+    nc = tc.nc
+    with ExitStack() as ctx:
+        ctx.enter_context(tc.manual_schedule())
+        const = ctx.enter_context(tc.tile_pool(name="const", bufs=1))
+        inp = ctx.enter_context(tc.tile_pool(name="inp", bufs=1))
+        work = ctx.enter_context(tc.tile_pool(name="work", bufs=3))
+        outp = ctx.enter_context(tc.tile_pool(name="outp", bufs=4))
+        pt = ctx.enter_context(tc.psum_pool(name="pt", bufs=2))
+        ps = ctx.enter_context(tc.psum_pool(name="ps", bufs=4))
+        po = ctx.enter_context(tc.psum_pool(name="po", bufs=2))
+
+        q_sb, k_sb, v_sb = [], [], []
+        for b in range(B):
+            q_sb.append(inp.tile([P, H, 4 * D], BF16, name="q_sb%d" % b))
+            k_sb.append(inp.tile([P, H * 4, D], BF16, name="k_sb%d" % b))
+            v_sb.append(inp.tile([P, H * 4, D], BF16, name="v_sb%d" % b))
+        def load(b):
+            cuts = [(0, 1), (1, H)] if b == 0 else [(0, H)]
+            for h0, h1 in cuts:
+                nc.sync.dma_start(
+                    out=q_sb[b][:, h0:h1, :],
+                    in_=q_scaled[b, h0:h1].rearrange("h (m u) d -> m h (u d)", u=4),
+                )
+                nc.sync.dma_start(
+                    out=k_sb[b][:, 4 * h0 : 4 * h1, :],
+                    in_=k[b, h0:h1].rearrange("h (t p) d -> p (h t) d", p=P),
+                )
+                nc.sync.dma_start(
+                    out=v_sb[b][:, 4 * h0 : 4 * h1, :],
+                    in_=v[b, h0:h1].rearrange("h (t p) d -> p (h t) d", p=P),
+                )
+
+        for b in range(AHEAD):
+            load(b)
+
+        ident = const.tile([P, P], BF16, name="ident")
+        make_identity(nc, ident[:])
+        expo = const.tile([P, 512], F32, name="expo")
+        nc.gpsimd.iota(
+            expo[:],
+            pattern=[[1, 4], [4, 32], [-128, 4]],
+            base=384,
+            channel_multiplier=-1,
+            allow_small_or_imprecise_dtypes=True,
+        )
+        g_tiles = []
+        for i in range(NG):
+            g = const.tile([P, 2048], BF16, name="g%d" % i, align_bytes=64)
+            nc.vector.memset(g[:].bitcast(I32), 0)
+            g_tiles.append(g)
+        tabs = []
+        for h in range(H):
+            raw = const.tile([P, 512], F32, name="raw%d" % h)
+            nc.scalar.activation(out=raw[:], in_=expo[:], func=ACT.Exp, scale=math.log(1.0 - 2.0 ** (-5 - h)))
+            tab = const.tile([P, 512], F32, name="tab%d" % h)
+            nc.vector.scalar_tensor_tensor(
+                out=tab[:], in0=expo[:], scalar=0.0, in1=raw[:], op0=ALU.is_ge, op1=ALU.mult
+            )
+            tabs.append(tab)
+
+        qkT, s_ps, words, planes, vwords, vplanes, vgs = {}, {}, {}, {}, {}, {}, {}
+
+        def transposes(n):
+            b, h = divmod(n, H)
+            t_ps = pt.tile([P, 1024], BF16, name="t_ps")
+            for u in range(4):
+                nc.tensor.transpose(t_ps[:, 128 * u : 128 * u + 128], q_sb[b][:, h, 128 * u : 128 * u + 128], ident[:])
+            for t in range(4):
+                nc.tensor.transpose(t_ps[:, 512 + 128 * t : 640 + 128 * t], k_sb[b][:, 4 * h + t, :], ident[:])
+            qk = work.tile([P, 1024], BF16, name="qk")
+            nc.scalar.copy(out=qk[:], in_=t_ps[:])
+            qkT[n] = qk
+
+        def regroup_v(n):
+            b, h = divmod(n, H)
+            vg = work.tile([P, 512], BF16, name="vg", align_bytes=64)
+            nc.scalar.copy(
+                out=vg[:].rearrange("p (c i t) -> p c t i", i=4, t=4),
+                in_=v_sb[b][:, 4 * h : 4 * h + 4, :].rearrange("p t (c i) -> p c t i", i=4),
+            )
+            vgs[n] = vg
+
+        def quantise_v(n):
+            vw = work.tile([P, 128], U32, name="vw", align_bytes=64, bufs=4)
+            vp = work.tile([P, 128], U8, name="vp", align_bytes=64, bufs=4)
+            nc.vector.quantize_mx(out=vw[:].bitcast(FP8X4), scales=vp[:], in_=vgs[n][:])
+            vwords[n], vplanes[n] = vw, vp
+
+        def scores(n):
+            qk = qkT[n]
+            tiles = []
+            for i in range(3):
+                s = ps.tile([P, 4, 128], F32, name="s_ps")
+                tiles.append(s)
+            s_ps[n] = tiles
+            qv = qk[:, 0:512].rearrange("d (u m) -> d u m", u=4)
+            for ib in (3, 2, 0, 1):
+                which, slot = S_PLACE[ib]
+                for t in range(ib + 1):
+                    nc.tensor.matmul(
+                        out=tiles[which][:, slot + t, :].rearrange("p (u m) -> p u m", u=4),
+                        lhsT=qk[:, 512 + 128 * t : 640 + 128 * t],
+                        rhs=qv[:, :, 32 * ib : 32 * ib + 32],
+                        start=True,
+                        stop=True,
+                    )
+
+        def decay(n, ib):
+            h = n % H
+            which, slot = S_PLACE[ib]
+            gv = g_tiles[n % NG][:].rearrange("p (u m t) -> p u m t", u=4, t=4)
+            nc.vector.tensor_tensor(
+                out=gv[:, :, 32 * ib : 32 * ib + 32, 0 : ib + 1],
+                in0=s_ps[n][which][:, slot : slot + ib + 1, :].rearrange("p t (u m) -> p u m t", u=4),
+                in1=tabs[h][:].rearrange("p (u m s) -> p u m s", u=4, s=4)[:, :, :, 3 - ib : 4],
+                op=ALU.mult,
+            )
+
+        def quantise_p(n):
+            w = work.tile([P, 512], U32, name="w", align_bytes=64)
+            pl = work.tile([P, 512], U8, name="pl", align_bytes=64)
+            nc.vector.quantize_mx(out=w[:].bitcast(FP8X4), scales=pl[:], in_=g_tiles[n % NG][:])
+            words[n], planes[n] = w, pl
+
+        def second_matmul(n):
+            b, h = divmod(n, H)
+            o_ps = po.tile([P, 512], F32, name="o_ps")
+            for u in range(4):
+                cols = slice(128 * u, 128 * u + 128)
+                nc.tensor.matmul_mx(
+                    out=o_ps[:, cols],
+                    lhsT=words[n][:, cols].bitcast(FP8X4),
+                    lhsT_scale=planes[n][:, cols],
+                    rhs=vwords[n][:].bitcast(FP8X4),
+                    rhs_scale=vplanes[n][:],
+                    start=True,
+                    stop=True,
+                )
+            o_sb = outp.tile([P, 512], F32, name="o_sb")
+            nc.scalar.copy(out=o_sb[:], in_=o_ps[:])
+            nc.sync.dma_start(out=out[b, h].rearrange("(m u) d -> m (u d)", u=4), in_=o_sb[:])
+
+        def live(n):
+            return 0 <= n < NH
+
+        for it in range(-2, NH + 1):
+            if it >= 0 and it % H == 0 and it // H + AHEAD < B:
+                load(it // H + AHEAD)
+            if live(it + 2):
+                transposes(it + 2)
+                regroup_v(it + 2)
+            if live(it + 1):
+                scores(it + 1)
+            if live(it):
+                decay(it, 3)
+            if live(it - 1):
+                quantise_p(it - 1)
+            if live(it):
+                decay(it, 2)
+            if live(it + 1):
+                quantise_v(it + 1)
+            if live(it):
+                decay(it, 0)
+                decay(it, 1)
+            if live(it - 1):
+                second_matmul(it - 1)

@@ -18,9 +18,10 @@ FP8X4 = mybir.dt.float8_e4m3fn_x4
 ALU = mybir.AluOpType
 ACT = mybir.ActivationFunctionType
 
-S_PLACE = {3: (0, 0), 2: (1, 0), 0: (1, 3), 1: (2, 0)}
-NG = 3
+S_PLACE = {2: (0, 0), 0: (0, 3), 3: (1, 0), 1: (2, 0)}
+NG = 2
 AHEAD = 3
+ON_G = (0,)
 
 
 def tile_model_pa_t_kernel(tc, q_scaled, k, v, out):
@@ -40,6 +41,7 @@ def tile_model_pa_t_kernel(tc, q_scaled, k, v, out):
             q_sb.append(inp.tile([P, H, 4 * D], BF16, name="q_sb%d" % b))
             k_sb.append(inp.tile([P, H * 4, D], BF16, name="k_sb%d" % b))
             v_sb.append(inp.tile([P, H * 4, D], BF16, name="v_sb%d" % b))
+
         def load(b):
             cuts = [(0, 1), (1, H)] if b == 0 else [(0, H)]
             for h0, h1 in cuts:
@@ -74,17 +76,18 @@ def tile_model_pa_t_kernel(tc, q_scaled, k, v, out):
             g = const.tile([P, 2048], BF16, name="g%d" % i, align_bytes=64)
             nc.vector.memset(g[:].bitcast(I32), 0)
             g_tiles.append(g)
-        tabs = []
-        for h in range(H):
+        tabs = {}
+
+        def build_table(h):
             raw = const.tile([P, 512], F32, name="raw%d" % h)
             nc.scalar.activation(out=raw[:], in_=expo[:], func=ACT.Exp, scale=math.log(1.0 - 2.0 ** (-5 - h)))
             tab = const.tile([P, 512], F32, name="tab%d" % h)
             nc.vector.scalar_tensor_tensor(
                 out=tab[:], in0=expo[:], scalar=0.0, in1=raw[:], op0=ALU.is_ge, op1=ALU.mult
             )
-            tabs.append(tab)
+            tabs[h] = tab
 
-        qkT, s_ps, words, planes, vwords, vplanes, vgs = {}, {}, {}, {}, {}, {}, {}
+        qkT, s_ps, fed, words, planes, vwords, vplanes, vgs = {}, {}, {}, {}, {}, {}, {}, {}
 
         def transposes(n):
             b, h = divmod(n, H)
@@ -99,18 +102,23 @@ def tile_model_pa_t_kernel(tc, q_scaled, k, v, out):
 
         def regroup_v(n):
             b, h = divmod(n, H)
-            vg = work.tile([P, 512], BF16, name="vg", align_bytes=64)
+            if h == 0:
+                vg_new = work.tile([P, H, 512], BF16, name="vg", align_bytes=64, bufs=2)
+                vgs[b] = vg_new
             nc.scalar.copy(
-                out=vg[:].rearrange("p (c i t) -> p c t i", i=4, t=4),
+                out=vgs[b][:, h, :].rearrange("p (c i t) -> p c t i", i=4, t=4),
                 in_=v_sb[b][:, 4 * h : 4 * h + 4, :].rearrange("p t (c i) -> p c t i", i=4),
             )
-            vgs[n] = vg
 
-        def quantise_v(n):
-            vw = work.tile([P, 128], U32, name="vw", align_bytes=64, bufs=4)
-            vp = work.tile([P, 128], U8, name="vp", align_bytes=64, bufs=4)
-            nc.vector.quantize_mx(out=vw[:].bitcast(FP8X4), scales=vp[:], in_=vgs[n][:])
-            vwords[n], vplanes[n] = vw, vp
+        def quantise_v(b):
+            vw = work.tile([P, H, 128], U32, name="vw", align_bytes=64, bufs=3)
+            vp = work.tile([P, H, 128], U8, name="vp", align_bytes=64, bufs=3)
+            nc.vector.quantize_mx(
+                out=vw[:].rearrange("p h c -> p (h c)").bitcast(FP8X4),
+                scales=vp[:].rearrange("p h c -> p (h c)"),
+                in_=vgs[b][:].rearrange("p h c -> p (h c)"),
+            )
+            vwords[b], vplanes[b] = vw, vp
 
         def scores(n):
             qk = qkT[n]
@@ -120,7 +128,7 @@ def tile_model_pa_t_kernel(tc, q_scaled, k, v, out):
                 tiles.append(s)
             s_ps[n] = tiles
             qv = qk[:, 0:512].rearrange("d (u m) -> d u m", u=4)
-            for ib in (3, 2, 0, 1):
+            for ib in (2, 0, 3, 1):
                 which, slot = S_PLACE[ib]
                 for t in range(ib + 1):
                     nc.tensor.matmul(
@@ -131,13 +139,23 @@ def tile_model_pa_t_kernel(tc, q_scaled, k, v, out):
                         stop=True,
                     )
 
+        def feed(n, ib):
+            which, slot = S_PLACE[ib]
+            f = work.tile([P, ib + 1, 128], F32, name="fed%d" % ib)
+            nc.scalar.copy(out=f[:], in_=s_ps[n][which][:, slot : slot + ib + 1, :])
+            fed[(n, ib)] = f
+
         def decay(n, ib):
             h = n % H
             which, slot = S_PLACE[ib]
             gv = g_tiles[n % NG][:].rearrange("p (u m t) -> p u m t", u=4, t=4)
-            nc.vector.tensor_tensor(
+            if ib in ON_G:
+                eng, src = nc.gpsimd, fed[(n, ib)][:]
+            else:
+                eng, src = nc.vector, s_ps[n][which][:, slot : slot + ib + 1, :]
+            eng.tensor_tensor(
                 out=gv[:, :, 32 * ib : 32 * ib + 32, 0 : ib + 1],
-                in0=s_ps[n][which][:, slot : slot + ib + 1, :].rearrange("p t (u m) -> p u m t", u=4),
+                in0=src.rearrange("p t (u m) -> p u m t", u=4),
                 in1=tabs[h][:].rearrange("p (u m s) -> p u m s", u=4, s=4)[:, :, :, 3 - ib : 4],
                 op=ALU.mult,
             )
@@ -157,8 +175,8 @@ def tile_model_pa_t_kernel(tc, q_scaled, k, v, out):
                     out=o_ps[:, cols],
                     lhsT=words[n][:, cols].bitcast(FP8X4),
                     lhsT_scale=planes[n][:, cols],
-                    rhs=vwords[n][:].bitcast(FP8X4),
-                    rhs_scale=vplanes[n][:],
+                    rhs=vwords[b][:, h, :].bitcast(FP8X4),
+                    rhs_scale=vplanes[b][:, h, :],
                     start=True,
                     stop=True,
                 )
@@ -169,24 +187,34 @@ def tile_model_pa_t_kernel(tc, q_scaled, k, v, out):
         def live(n):
             return 0 <= n < NH
 
+        REGROUP = {2: (2,), 3: (2, 3), 0: (3,), 1: ()}
+
         for it in range(-2, NH + 1):
             if it >= 0 and it % H == 0 and it // H + AHEAD < B:
                 load(it // H + AHEAD)
             if live(it + 2):
                 transposes(it + 2)
-                regroup_v(it + 2)
+                if it + 2 < H:
+                    build_table(it + 2)
+            for ahead in REGROUP[it % 4]:
+                if live(it + ahead):
+                    regroup_v(it + ahead)
             if live(it + 1):
                 scores(it + 1)
-            if live(it):
-                decay(it, 3)
-            if live(it - 1):
-                quantise_p(it - 1)
+                for ib in ON_G:
+                    feed(it + 1, ib)
             if live(it):
                 decay(it, 2)
+            if it % H == 1 and live(it):
+                quantise_v(it // H)
+            if live(it - 1):
+                quantise_p(it - 1)
             if live(it + 1):
-                quantise_v(it + 1)
+                for ib in ON_G:
+                    decay(it + 1, ib)
             if live(it):
-                decay(it, 0)
-                decay(it, 1)
+                for ib in (3, 1, 0):
+                    if ib not in ON_G:
+                        decay(it, ib)
             if live(it - 1):
                 second_matmul(it - 1)

@@ -18,7 +18,7 @@ FP8X4 = mybir.dt.float8_e4m3fn_x4
 ALU = mybir.AluOpType
 ACT = mybir.ActivationFunctionType
 
-S_PLACE = {2: (0, 0), 0: (0, 3), 3: (1, 0), 1: (2, 0)}
+S_PLACE = {2: (0, 0), 3: (1, 0), 1: (2, 0), 0: (2, 2)}
 NG = 2
 AHEAD = 3
 ON_G = (0,)
@@ -128,7 +128,7 @@ def tile_model_pa_t_kernel(tc, q_scaled, k, v, out):
                 tiles.append(s)
             s_ps[n] = tiles
             qv = qk[:, 0:512].rearrange("d (u m) -> d u m", u=4)
-            for ib in (2, 0, 3, 1):
+            for ib in (2, 3, 1, 0):
                 which, slot = S_PLACE[ib]
                 for t in range(ib + 1):
                     nc.tensor.matmul(
@@ -161,8 +161,8 @@ def tile_model_pa_t_kernel(tc, q_scaled, k, v, out):
             )
 
         def quantise_p(n):
-            w = work.tile([P, 512], U32, name="w", align_bytes=64)
-            pl = work.tile([P, 512], U8, name="pl", align_bytes=64)
+            w = work.tile([P, 512], U32, name="w", align_bytes=64, bufs=4)
+            pl = work.tile([P, 512], U8, name="pl", align_bytes=64, bufs=4)
             nc.vector.quantize_mx(out=w[:].bitcast(FP8X4), scales=pl[:], in_=g_tiles[n % NG][:])
             words[n], planes[n] = w, pl
 
@@ -189,32 +189,29 @@ def tile_model_pa_t_kernel(tc, q_scaled, k, v, out):
 
         REGROUP = {2: (2,), 3: (2, 3), 0: (3,), 1: ()}
 
-        for it in range(-2, NH + 1):
+        for it in range(-2, NH + 2):
             if it >= 0 and it % H == 0 and it // H + AHEAD < B:
                 load(it // H + AHEAD)
+            if live(it - 2):
+                second_matmul(it - 2)
             if live(it + 2):
                 transposes(it + 2)
                 if it + 2 < H:
                     build_table(it + 2)
-            for ahead in REGROUP[it % 4]:
-                if live(it + ahead):
-                    regroup_v(it + ahead)
             if live(it + 1):
                 scores(it + 1)
                 for ib in ON_G:
                     feed(it + 1, ib)
+            for ahead in REGROUP[it % 4]:
+                if live(it + ahead):
+                    regroup_v(it + ahead)
             if live(it):
                 decay(it, 2)
+                decay(it, 3)
             if it % H == 1 and live(it):
                 quantise_v(it // H)
             if live(it - 1):
                 quantise_p(it - 1)
-            if live(it + 1):
-                for ib in ON_G:
-                    decay(it + 1, ib)
             if live(it):
-                for ib in (3, 1, 0):
-                    if ib not in ON_G:
-                        decay(it, ib)
-            if live(it - 1):
-                second_matmul(it - 1)
+                decay(it, 1)
+                decay(it, 0)

@@ -19,7 +19,7 @@ ALU = mybir.AluOpType
 ACT = mybir.ActivationFunctionType
 
 S_PLACE = {2: (0, 0), 3: (1, 0), 1: (2, 0), 0: (2, 2)}
-NG = 2
+NG = 3
 AHEAD = 3
 ON_G = (0,)
 
@@ -189,14 +189,15 @@ def tile_model_pa_t_kernel(tc, q_scaled, k, v, out):
 
         REGROUP = {2: (2,), 3: (2, 3), 0: (3,), 1: ()}
 
-        for it in range(-2, NH + 2):
+        build_table(0)
+        for it in range(-2, NH + 3):
             if it >= 0 and it % H == 0 and it // H + AHEAD < B:
                 load(it // H + AHEAD)
-            if live(it - 2):
-                second_matmul(it - 2)
+            if live(it - 3):
+                second_matmul(it - 3)
             if live(it + 2):
                 transposes(it + 2)
-                if it + 2 < H:
+                if 0 < it + 2 < H:
                     build_table(it + 2)
             if live(it + 1):
                 scores(it + 1)
@@ -210,8 +211,8 @@ def tile_model_pa_t_kernel(tc, q_scaled, k, v, out):
                 decay(it, 3)
             if it % H == 1 and live(it):
                 quantise_v(it // H)
-            if live(it - 1):
-                quantise_p(it - 1)
+            if live(it - 2):
+                quantise_p(it - 2)
             if live(it):
                 decay(it, 1)
                 decay(it, 0)

@@ -209,10 +209,9 @@ def tile_model_pa_t_kernel(tc, q_scaled, k, v, out):
             if live(it):
                 decay(it, 2)
                 decay(it, 3)
-            if it % H == 1 and live(it):
-                quantise_v(it // H)
-            if live(it - 2):
-                quantise_p(it - 2)
-            if live(it):
                 decay(it, 1)
                 decay(it, 0)
+            if live(it - 2):
+                quantise_p(it - 2)
+            if it % H == 1 and live(it):
+                quantise_v(it // H)

@@ -18,10 +18,10 @@ FP8X4 = mybir.dt.float8_e4m3fn_x4
 ALU = mybir.AluOpType
 ACT = mybir.ActivationFunctionType
 
-S_PLACE = {2: (0, 0), 3: (1, 0), 1: (2, 0), 0: (2, 2)}
 NG = 3
 AHEAD = 3
-ON_G = (0,)
+LOW = ((1, 0), (1, 1), (0, 0))
+KEY_BLOCK = (0, 2, 1, 3)
 
 
 def tile_model_pa_t_kernel(tc, q_scaled, k, v, out):
@@ -33,7 +33,7 @@ def tile_model_pa_t_kernel(tc, q_scaled, k, v, out):
         work = ctx.enter_context(tc.tile_pool(name="work", bufs=3))
         outp = ctx.enter_context(tc.tile_pool(name="outp", bufs=4))
         pt = ctx.enter_context(tc.psum_pool(name="pt", bufs=2))
-        ps = ctx.enter_context(tc.psum_pool(name="ps", bufs=4))
+        ps = ctx.enter_context(tc.psum_pool(name="ps", bufs=1))
         po = ctx.enter_context(tc.psum_pool(name="po", bufs=2))
 
         q_sb, k_sb, v_sb = [], [], []
@@ -66,28 +66,48 @@ def tile_model_pa_t_kernel(tc, q_scaled, k, v, out):
         expo = const.tile([P, 512], F32, name="expo")
         nc.gpsimd.iota(
             expo[:],
-            pattern=[[1, 4], [4, 32], [-128, 4]],
+            pattern=[[1, 4], [4, 32], [-128, 2], [-256, 2]],
             base=384,
             channel_multiplier=-1,
             allow_small_or_imprecise_dtypes=True,
         )
+        zeros = const.tile([P, 512], BF16, name="zeros")
+        nc.vector.memset(zeros[:].bitcast(I32), 0)
         g_tiles = []
         for i in range(NG):
             g = const.tile([P, 2048], BF16, name="g%d" % i, align_bytes=64)
             nc.vector.memset(g[:].bitcast(I32), 0)
             g_tiles.append(g)
-        tabs = {}
+        z_ps = ps.tile([P, 1024], BF16, name="z_ps")
+        for half in range(2):
+            nc.tensor.matmul(
+                out=z_ps[:, 512 * half : 512 * half + 512], lhsT=ident[:], rhs=zeros[:], start=True, stop=True
+            )
+        zv = z_ps[:].rearrange("p (u m t) -> p u m t", u=4, t=4)
+        tabs, low_tabs = {}, {}
 
         def build_table(h):
-            raw = const.tile([P, 512], F32, name="raw%d" % h)
-            nc.scalar.activation(out=raw[:], in_=expo[:], func=ACT.Exp, scale=math.log(1.0 - 2.0 ** (-5 - h)))
-            tab = const.tile([P, 512], F32, name="tab%d" % h)
-            nc.vector.scalar_tensor_tensor(
-                out=tab[:], in0=expo[:], scalar=0.0, in1=raw[:], op0=ALU.is_ge, op1=ALU.mult
-            )
-            tabs[h] = tab
+            log_gamma = math.log(1.0 - 2.0 ** (-5 - h))
+            for ib in (3, 2):
+                shift = 128.0 * (3 - ib)
+                raw = const.tile([P, 512], F32, name="raw%d_%d" % (h, ib))
+                nc.scalar.activation(out=raw[:], in_=expo[:], func=ACT.Exp, scale=log_gamma, bias=-shift * log_gamma)
+                tab = const.tile([P, 128, 4], F32, name="tab%d_%d" % (h, ib))
+                nc.vector.scalar_tensor_tensor(
+                    out=tab[:].rearrange("p c s -> p (c s)"),
+                    in0=expo[:],
+                    scalar=shift,
+                    in1=raw[:],
+                    op0=ALU.is_ge,
+                    op1=ALU.mult,
+                )
+                tabs[(h, ib)] = tab
+            low = const.tile([P, 3, 128], F32, name="low%d" % h)
+            for i, (ib, jb) in enumerate(LOW):
+                nc.vector.tensor_copy(out=low[:, i, :], in_=tabs[(h, 3)][:, :, KEY_BLOCK.index(3 - ib + jb)])
+            low_tabs[h] = low
 
-        qkT, s_ps, fed, words, planes, vwords, vplanes, vgs = {}, {}, {}, {}, {}, {}, {}, {}
+        qkT, s_ps, packed, words, planes, vwords, vplanes, vgs = {}, {}, {}, {}, {}, {}, {}, {}
 
         def transposes(n):
             b, h = divmod(n, H)
@@ -106,8 +126,8 @@ def tile_model_pa_t_kernel(tc, q_scaled, k, v, out):
                 vg_new = work.tile([P, H, 512], BF16, name="vg", align_bytes=64, bufs=2)
                 vgs[b] = vg_new
             nc.scalar.copy(
-                out=vgs[b][:, h, :].rearrange("p (c i t) -> p c t i", i=4, t=4),
-                in_=v_sb[b][:, 4 * h : 4 * h + 4, :].rearrange("p t (c i) -> p c t i", i=4),
+                out=vgs[b][:, h, :].rearrange("p (d y x) -> p d y x", y=2, x=2),
+                in_=v_sb[b][:, 4 * h : 4 * h + 4, :].rearrange("p (x y) d -> p d y x", x=2),
             )
 
         def quantise_v(b):
@@ -120,44 +140,56 @@ def tile_model_pa_t_kernel(tc, q_scaled, k, v, out):
             )
             vwords[b], vplanes[b] = vw, vp
 
-        def scores(n):
+        def score_block(n, dst, ib, t):
             qk = qkT[n]
-            tiles = []
-            for i in range(3):
-                s = ps.tile([P, 4, 128], F32, name="s_ps")
-                tiles.append(s)
-            s_ps[n] = tiles
-            qv = qk[:, 0:512].rearrange("d (u m) -> d u m", u=4)
-            for ib in (2, 3, 1, 0):
-                which, slot = S_PLACE[ib]
-                for t in range(ib + 1):
-                    nc.tensor.matmul(
-                        out=tiles[which][:, slot + t, :].rearrange("p (u m) -> p u m", u=4),
-                        lhsT=qk[:, 512 + 128 * t : 640 + 128 * t],
-                        rhs=qv[:, :, 32 * ib : 32 * ib + 32],
-                        start=True,
-                        stop=True,
-                    )
+            nc.tensor.matmul(
+                out=dst.rearrange("p (u m) -> p u m", u=4),
+                lhsT=qk[:, 512 + 128 * t : 640 + 128 * t],
+                rhs=qk[:, 0:512].rearrange("d (u m) -> d u m", u=4)[:, :, 32 * ib : 32 * ib + 32],
+                start=True,
+                stop=True,
+            )
 
-        def feed(n, ib):
-            which, slot = S_PLACE[ib]
-            f = work.tile([P, ib + 1, 128], F32, name="fed%d" % ib)
-            nc.scalar.copy(out=f[:], in_=s_ps[n][which][:, slot : slot + ib + 1, :])
-            fed[(n, ib)] = f
+        def scores_high(n, ib):
+            s = ps.tile([P, ib + 1, 128], F32, name="s%d" % ib)
+            for t in range(ib + 1):
+                score_block(n, s[:, t, :], ib, KEY_BLOCK[t])
+            s_ps[(n, ib)] = s
 
-        def decay(n, ib):
-            h = n % H
-            which, slot = S_PLACE[ib]
+        def scores_low(n):
+            s = ps.tile([P, 3, 128], F32, name="slow")
+            for i, (ib, t) in enumerate(LOW):
+                score_block(n, s[:, i, :], ib, t)
+            s_ps[(n, 0)] = s
+
+        def decay_high(n, ib):
             gv = g_tiles[n % NG][:].rearrange("p (u m t) -> p u m t", u=4, t=4)
-            if ib in ON_G:
-                eng, src = nc.gpsimd, fed[(n, ib)][:]
-            else:
-                eng, src = nc.vector, s_ps[n][which][:, slot : slot + ib + 1, :]
-            eng.tensor_tensor(
+            nc.vector.tensor_tensor(
                 out=gv[:, :, 32 * ib : 32 * ib + 32, 0 : ib + 1],
-                in0=src.rearrange("p t (u m) -> p u m t", u=4),
-                in1=tabs[h][:].rearrange("p (u m s) -> p u m s", u=4, s=4)[:, :, :, 3 - ib : 4],
+                in0=s_ps[(n, ib)][:].rearrange("p t (u m) -> p u m t", u=4),
+                in1=tabs[(n % H, ib)][:].rearrange("p (u m) s -> p u m s", u=4)[:, :, :, 0 : ib + 1],
                 op=ALU.mult,
+            )
+
+        def decay_low(n):
+            c = work.tile([P, 3, 128], BF16, name="c")
+            nc.vector.tensor_tensor(out=c[:], in0=s_ps[(n, 0)][:], in1=low_tabs[n % H][:], op=ALU.mult)
+            packed[n] = c
+
+        def spread_low(n):
+            for i, (ib, t) in enumerate(LOW):
+                nc.tensor.matmul(
+                    out=zv[:, :, 32 * ib : 32 * ib + 32, KEY_BLOCK.index(t)],
+                    lhsT=ident[:],
+                    rhs=packed[n][:, i, :].rearrange("p (u m) -> p u m", u=4),
+                    start=True,
+                    stop=True,
+                )
+
+        def copy_low(n):
+            nc.scalar.copy(
+                out=g_tiles[n % NG][:].rearrange("p (u x) -> p u x", u=4)[:, :, 0:256],
+                in_=z_ps[:].rearrange("p (u x) -> p u x", u=4),
             )
 
         def quantise_p(n):
@@ -193,25 +225,29 @@ def tile_model_pa_t_kernel(tc, q_scaled, k, v, out):
         for it in range(-2, NH + 3):
             if it >= 0 and it % H == 0 and it // H + AHEAD < B:
                 load(it // H + AHEAD)
+            if live(it - 1):
+                copy_low(it - 1)
             if live(it - 3):
                 second_matmul(it - 3)
             if live(it + 2):
                 transposes(it + 2)
                 if 0 < it + 2 < H:
                     build_table(it + 2)
-            if live(it + 1):
-                scores(it + 1)
-                for ib in ON_G:
-                    feed(it + 1, ib)
             for ahead in REGROUP[it % 4]:
                 if live(it + ahead):
                     regroup_v(it + ahead)
             if live(it):
-                decay(it, 2)
-                decay(it, 3)
-                decay(it, 1)
-                decay(it, 0)
+                decay_high(it, 2)
+                decay_high(it, 3)
+                decay_low(it)
             if live(it - 2):
                 quantise_p(it - 2)
             if it % H == 1 and live(it):
                 quantise_v(it // H)
+            if live(it + 1):
+                scores_high(it + 1, 2)
+                scores_high(it + 1, 3)
+            if live(it):
+                spread_low(it)
+            if live(it + 1):
+                scores_low(it + 1)

import math
from contextlib import ExitStack

import concourse.mybir as mybir
from concourse.masks import make_identity

B, H, L, D = 8, 4, 512, 128
P = 128
NH = B * H
FLOPS = 4 * B * H * L * L * D

BF16 = mybir.dt.bfloat16
F32 = mybir.dt.float32
I32 = mybir.dt.int32
U32 = mybir.dt.uint32
U8 = mybir.dt.uint8
FP8X4 = mybir.dt.float8_e4m3fn_x4
ALU = mybir.AluOpType
ACT = mybir.ActivationFunctionType

NG = 3
AHEAD = 3
LOW = ((1, 0), (1, 1), (0, 0))
KEY_BLOCK = (0, 2, 1, 3)


def tile_model_pa_t_kernel(tc, q_scaled, k, v, out):
    nc = tc.nc
    with ExitStack() as ctx:
        ctx.enter_context(tc.manual_schedule())
        const = ctx.enter_context(tc.tile_pool(name="const", bufs=1))
        inp = ctx.enter_context(tc.tile_pool(name="inp", bufs=1))
        work = ctx.enter_context(tc.tile_pool(name="work", bufs=3))
        outp = ctx.enter_context(tc.tile_pool(name="outp", bufs=4))
        pt = ctx.enter_context(tc.psum_pool(name="pt", bufs=2))
        ps = ctx.enter_context(tc.psum_pool(name="ps", bufs=1))
        po = ctx.enter_context(tc.psum_pool(name="po", bufs=2))

        q_sb, k_sb, v_sb = [], [], []
        for b in range(B):
            q_sb.append(inp.tile([P, H, 4 * D], BF16, name="q_sb%d" % b))
            k_sb.append(inp.tile([P, H * 4, D], BF16, name="k_sb%d" % b))
            v_sb.append(inp.tile([P, H * 4, D], BF16, name="v_sb%d" % b))

        def load(b):
            cuts = [(0, 1), (1, H)] if b == 0 else [(0, H)]
            for h0, h1 in cuts:
                nc.sync.dma_start(
                    out=q_sb[b][:, h0:h1, :],
                    in_=q_scaled[b, h0:h1].rearrange("h (m u) d -> m h (u d)", u=4),
                )
                nc.sync.dma_start(
                    out=k_sb[b][:, 4 * h0 : 4 * h1, :],
                    in_=k[b, h0:h1].rearrange("h (t p) d -> p (h t) d", p=P),
                )
                nc.sync.dma_start(
                    out=v_sb[b][:, 4 * h0 : 4 * h1, :],
                    in_=v[b, h0:h1].rearrange("h (t p) d -> p (h t) d", p=P),
                )

        for b in range(AHEAD):
            load(b)

        ident = const.tile([P, P], BF16, name="ident")
        make_identity(nc, ident[:])
        expo = const.tile([P, 512], F32, name="expo")
        nc.gpsimd.iota(
            expo[:],
            pattern=[[1, 4], [4, 32], [-128, 2], [-256, 2]],
            base=384,
            channel_multiplier=-1,
            allow_small_or_imprecise_dtypes=True,
        )
        zeros = const.tile([P, 512], BF16, name="zeros")
        nc.vector.memset(zeros[:].bitcast(I32), 0)
        g_tiles = []
        for i in range(NG):
            g = const.tile([P, 2048], BF16, name="g%d" % i, align_bytes=64)
            nc.vector.memset(g[:].bitcast(I32), 0)
            g_tiles.append(g)
        z_ps = ps.tile([P, 1024], BF16, name="z_ps")
        for half in range(2):
            nc.tensor.matmul(
                out=z_ps[:, 512 * half : 512 * half + 512], lhsT=ident[:], rhs=zeros[:], start=True, stop=True
            )
        zv = z_ps[:].rearrange("p (u m t) -> p u m t", u=4, t=4)
        tabs, low_tabs = {}, {}

        def build_table(h):
            log_gamma = math.log(1.0 - 2.0 ** (-5 - h))
            for ib in (3, 2):
                shift = 128.0 * (3 - ib)
                raw = const.tile([P, 512], F32, name="raw%d_%d" % (h, ib))
                nc.scalar.activation(out=raw[:], in_=expo[:], func=ACT.Exp, scale=log_gamma, bias=-shift * log_gamma)
                tab = const.tile([P, 128, 4], F32, name="tab%d_%d" % (h, ib))
                nc.vector.scalar_tensor_tensor(
                    out=tab[:].rearrange("p c s -> p (c s)"),
                    in0=expo[:],
                    scalar=shift,
                    in1=raw[:],
                    op0=ALU.is_ge,
                    op1=ALU.mult,
                )
                tabs[(h, ib)] = tab
            low = const.tile([P, 3, 128], F32, name="low%d" % h)
            for i, (ib, jb) in enumerate(LOW):
                nc.vector.tensor_copy(out=low[:, i, :], in_=tabs[(h, 3)][:, :, KEY_BLOCK.index(3 - ib + jb)])
            low_tabs[h] = low

        qkT, s_ps, packed, words, planes, vwords, vplanes, vgs = {}, {}, {}, {}, {}, {}, {}, {}

        def transposes(n):
            b, h = divmod(n, H)
            t_ps = pt.tile([P, 1024], BF16, name="t_ps")
            for u in range(4):
                nc.tensor.transpose(t_ps[:, 128 * u : 128 * u + 128], q_sb[b][:, h, 128 * u : 128 * u + 128], ident[:])
            for t in range(4):
                nc.tensor.transpose(t_ps[:, 512 + 128 * t : 640 + 128 * t], k_sb[b][:, 4 * h + t, :], ident[:])
            qk = work.tile([P, 1024], BF16, name="qk")
            nc.scalar.copy(out=qk[:], in_=t_ps[:])
            qkT[n] = qk

        def regroup_v(n):
            b, h = divmod(n, H)
            if h == 0:
                vg_new = work.tile([P, H, 512], BF16, name="vg", align_bytes=64, bufs=2)
                vgs[b] = vg_new
            nc.scalar.copy(
                out=vgs[b][:, h, :].rearrange("p (d y x) -> p d y x", y=2, x=2),
                in_=v_sb[b][:, 4 * h : 4 * h + 4, :].rearrange("p (x y) d -> p d y x", x=2),
            )

        def quantise_v(b):
            vw = work.tile([P, H, 128], U32, name="vw", align_bytes=64, bufs=3)
            vp = work.tile([P, H, 128], U8, name="vp", align_bytes=64, bufs=3)
            nc.vector.quantize_mx(
                out=vw[:].rearrange("p h c -> p (h c)").bitcast(FP8X4),
                scales=vp[:].rearrange("p h c -> p (h c)"),
                in_=vgs[b][:].rearrange("p h c -> p (h c)"),
            )
            vwords[b], vplanes[b] = vw, vp

        def score_block(n, dst, ib, t):
            qk = qkT[n]
            nc.tensor.matmul(
                out=dst.rearrange("p (u m) -> p u m", u=4),
                lhsT=qk[:, 512 + 128 * t : 640 + 128 * t],
                rhs=qk[:, 0:512].rearrange("d (u m) -> d u m", u=4)[:, :, 32 * ib : 32 * ib + 32],
                start=True,
                stop=True,
            )

        def scores_high(n, ib):
            s = ps.tile([P, ib + 1, 128], F32, name="s%d" % ib)
            for t in range(ib + 1):
                score_block(n, s[:, t, :], ib, KEY_BLOCK[t])
            s_ps[(n, ib)] = s

        def scores_low(n):
            s = ps.tile([P, 3, 128], F32, name="slow")
            for i, (ib, t) in enumerate(LOW):
                score_block(n, s[:, i, :], ib, t)
            s_ps[(n, 0)] = s

        def decay_high(n, ib):
            gv = g_tiles[n % NG][:].rearrange("p (u m t) -> p u m t", u=4, t=4)
            nc.vector.tensor_tensor(
                out=gv[:, :, 32 * ib : 32 * ib + 32, 0 : ib + 1],
                in0=s_ps[(n, ib)][:].rearrange("p t (u m) -> p u m t", u=4),
                in1=tabs[(n % H, ib)][:].rearrange("p (u m) s -> p u m s", u=4)[:, :, :, 0 : ib + 1],
                op=ALU.mult,
            )

        def decay_low(n):
            c = work.tile([P, 3, 128], BF16, name="c")
            nc.vector.tensor_tensor(out=c[:], in0=s_ps[(n, 0)][:], in1=low_tabs[n % H][:], op=ALU.mult)
            packed[n] = c

        def spread_low(n):
            for i, (ib, t) in enumerate(LOW):
                nc.tensor.matmul(
                    out=zv[:, :, 32 * ib : 32 * ib + 32, KEY_BLOCK.index(t)],
                    lhsT=ident[:],
                    rhs=packed[n][:, i, :].rearrange("p (u m) -> p u m", u=4),
                    start=True,
                    stop=True,
                )

        def copy_low(n):
            nc.scalar.copy(
                out=g_tiles[n % NG][:].rearrange("p (u x) -> p u x", u=4)[:, :, 0:256],
                in_=z_ps[:].rearrange("p (u x) -> p u x", u=4),
            )

        def quantise_p(n):
            w = work.tile([P, 512], U32, name="w", align_bytes=64, bufs=4)
            pl = work.tile([P, 512], U8, name="pl", align_bytes=64, bufs=4)
            nc.vector.quantize_mx(out=w[:].bitcast(FP8X4), scales=pl[:], in_=g_tiles[n % NG][:])
            words[n], planes[n] = w, pl

        def second_matmul(n):
            b, h = divmod(n, H)
            o_ps = po.tile([P, 512], F32, name="o_ps")
            for u in range(4):
                cols = slice(128 * u, 128 * u + 128)
                nc.tensor.matmul_mx(
                    out=o_ps[:, cols],
                    lhsT=words[n][:, cols].bitcast(FP8X4),
                    lhsT_scale=planes[n][:, cols],
                    rhs=vwords[b][:, h, :].bitcast(FP8X4),
                    rhs_scale=vplanes[b][:, h, :],
                    start=True,
                    stop=True,
                )
            o_sb = outp.tile([P, 512], F32, name="o_sb")
            nc.scalar.copy(out=o_sb[:], in_=o_ps[:])
            nc.sync.dma_start(out=out[b, h].rearrange("(m u) d -> m (u d)", u=4), in_=o_sb[:])

        def live(n):
            return 0 <= n < NH

        REGROUP = {2: (2,), 3: (2, 3), 0: (3,), 1: ()}

        build_table(0)
        for it in range(-2, NH + 3):
            if it >= 0 and it % H == 0 and it // H + AHEAD < B:
                load(it // H + AHEAD)
            if live(it - 1):
                copy_low(it - 1)
            if live(it - 3):
                second_matmul(it - 3)
            if live(it + 2):
                transposes(it + 2)
                if 0 < it + 2 < H:
                    build_table(it + 2)
            for ahead in REGROUP[it % 4]:
                if live(it + ahead):
                    regroup_v(it + ahead)
            if live(it):
                decay_high(it, 2)
                decay_high(it, 3)
                decay_low(it)
            if live(it - 2):
                quantise_p(it - 2)
            if it % H == 1 and live(it):
                quantise_v(it // H)
            if live(it + 1):
                scores_high(it + 1, 2)
                scores_high(it + 1, 3)
            if live(it):
                spread_low(it)
            if live(it + 1):
                scores_low(it + 1)
